import numpy as np
import ml_dtypes


def mxq(x, axis, fmt="e4m3"):
    dtype, down = {"e4m3": (ml_dtypes.float8_e4m3fn, 7), "e5m2": (ml_dtypes.float8_e5m2, 14)}[fmt]
    v = np.moveaxis(np.asarray(x, np.float32).astype(ml_dtypes.bfloat16).astype(np.float64), axis, -1)
    blocks = v.reshape(v.shape[:-1] + (-1, 32))
    amax = np.abs(blocks).max(-1, keepdims=True)
    byte = np.maximum(np.where(amax > 0, np.frexp(amax)[1] - 1 + 127, 0) - down, 1)
    scale = np.exp2(byte - 127.0)
    codes = (blocks / scale).astype(np.float32).astype(dtype).astype(np.float64)
    return np.moveaxis((codes * scale).reshape(v.shape), -1, axis)


WIDE = False


def mx_kscale(k):
    if not WIDE:
        return np.ones(k)
    levels = np.array([10, -10, 5, -5, 0])
    a = np.random.permutation(np.resize(levels, k // 512 * 4)).reshape(k // 512, 4)
    idx = np.arange(k)
    return np.exp2(a[idx // 512, idx % 128 // 32])


BF16 = ml_dtypes.bfloat16


def bf(x):
    return np.asarray(x, np.float32).astype(BF16)


def f64(x):
    return np.asarray(x).astype(np.float64)


B, S, DIM, QK, EXP, V, G = 16, 1024, 512, 32, 32, 16, 512
W = 2 * QK + 2 * EXP
EPS = 1e-5
ERF_TERMS = 100


def erf(z):
    a = np.minimum(np.abs(z), 6.0)
    a2 = 2.0 * a * a
    term = a.copy()
    tot = a.copy()
    for n in range(1, ERF_TERMS):
        term *= a2
        term /= 2 * n + 1
        tot += term
    return np.sign(z) * 2.0 / np.sqrt(np.pi) * np.exp(-a * a) * tot


def gelu_erf(v):
    return 0.5 * v * (1.0 + erf(v / np.sqrt(2.0)))


def setup_inputs():
    s = mx_kscale(DIM)
    rows = np.exp2(np.random.uniform(-8.0, 1.0, (B, S, 1)))
    off = 0.5 * np.random.standard_normal((B, S, 1))
    gain = np.where(np.arange(W) < 2 * QK, 1.5, 1.0)[:, None]
    return {"x": bf((np.random.standard_normal((B, S, DIM)) + off) * rows),
            "norm_w": bf((1.0 + 0.1 * np.random.standard_normal(DIM)) * s),
            "expand_w": bf(np.random.standard_normal((W, DIM)) * gain / np.sqrt(DIM) / s)}


def reference(x, norm_w, expand_w):
    x = f64(x)
    mu = x.mean(-1, keepdims=True)
    var = ((x - mu) ** 2).mean(-1, keepdims=True)
    h = (x - mu) * (1.0 / np.sqrt(var + EPS)) * f64(norm_w)
    proj = mxq(h, 2, "e4m3") @ mxq(f64(expand_w), 1, "e4m3").T
    q = proj[..., :QK]
    k = proj[..., QK:2 * QK]
    lin = proj[..., 2 * QK:2 * QK + EXP]
    pre = proj[..., 2 * QK + EXP:]
    geglu = lin * gelu_erf(pre)
    return q, k, geglu[..., :EXP - V], geglu[..., EXP - V:]

@@ -1,0 +1,253 @@
+from contextlib import ExitStack
+
+import concourse.mybir as mybir
+from concourse.masks import make_identity
+
+F32 = mybir.dt.float32
+BF16 = mybir.dt.bfloat16
+U32 = mybir.dt.uint32
+U8 = mybir.dt.uint8
+FP8X4 = mybir.dt.float8_e4m3fn_x4
+ALU = mybir.AluOpType
+ACT = mybir.ActivationFunctionType
+
+P = 128
+PACK = 4
+TOKENS = 16 * 1024
+DIM = 512
+QK = 32
+EXP = 32
+HALF_EXP = 16
+WIDTH = 2 * QK + 2 * EXP
+EPS = 1e-5
+TILES = TOKENS // P
+QUAD = 4
+QUADS = TILES // QUAD
+
+FLOPS = 2 * TOKENS * DIM * WIDTH
+
+
+def turn_rows(nc, turned, rows, identity):
+    for j in range(PACK):
+        nc.tensor.transpose(turned[:, j, :], rows[:, j * P : (j + 1) * P], identity)
+
+
+def tile_latentattentionblock_pa_t_kernel(tc, x, norm_w, expand_w, out_0, out_1, out_2, out_3):
+    nc = tc.nc
+    x_rows = x.flatten_outer_dims().rearrange("(p i) d -> p i d", p=P)
+    q_rows = out_0.flatten_outer_dims().rearrange("(p i) c -> p i c", p=P)
+    k_rows = out_1.flatten_outer_dims().rearrange("(p i) c -> p i c", p=P)
+    gl_rows = out_2.flatten_outer_dims().rearrange("(p i) c -> p i c", p=P)
+    gv_rows = out_3.flatten_outer_dims().rearrange("(p i) c -> p i c", p=P)
+
+    with ExitStack() as ctx:
+        const = ctx.enter_context(tc.tile_pool(name="const", bufs=1))
+        x_pool = ctx.enter_context(tc.tile_pool(name="x", bufs=QUADS))
+        stat_pool = ctx.enter_context(tc.tile_pool(name="stat", bufs=6))
+        unread_pool = ctx.enter_context(tc.tile_pool(name="unread", bufs=6))
+        y_pool = ctx.enter_context(tc.tile_pool(name="y", bufs=8))
+        mx_pool = ctx.enter_context(tc.tile_pool(name="mx", bufs=3))
+        out_pool = ctx.enter_context(tc.tile_pool(name="out", bufs=4))
+        turned_pool = ctx.enter_context(tc.psum_pool(name="turned", bufs=6))
+        proj_pool = ctx.enter_context(tc.psum_pool(name="proj", bufs=2))
+
+        w_rows = const.tile([P, DIM], BF16)
+        nc.scalar.dma_start(out=w_rows[:], in_=expand_w)
+        gain_rows = const.tile([P, P], BF16)
+        nc.vector.memset(gain_rows[:], 0.0)
+        nc.scalar.dma_start(out=gain_rows[0:PACK, :], in_=norm_w.rearrange("(j c) -> j c", c=P))
+        x_quads = []
+        for q in range(QUADS):
+            x_quad = x_pool.tile([P, QUAD, DIM], BF16)
+            nc.sync.dma_start(out=x_quad[:], in_=x_rows[:, q * QUAD : (q + 1) * QUAD, :])
+            x_quads.append(x_quad)
+
+        identity = const.tile([P, P], F32)
+        make_identity(nc, identity[:])
+        minus_half = const.tile([P, QUAD], F32)
+        nc.vector.memset(minus_half[:], -0.5)
+
+        gain_rows_f = const.tile([P, P], F32)
+        nc.vector.tensor_copy(out=gain_rows_f[:], in_=gain_rows[:])
+        gain_turned = turned_pool.tile([P, PACK, P], F32, tag="turned")
+        nc.tensor.transpose(gain_turned[:, 0, :], gain_rows_f[:], identity[:])
+        gain = const.tile([P, PACK], F32)
+        nc.vector.tensor_copy(out=gain[:], in_=gain_turned[:, 0, 0:PACK])
+
+        w_rows_f = const.tile([P, DIM], F32)
+        nc.vector.tensor_copy(out=w_rows_f[:], in_=w_rows[:])
+        w_turned = turned_pool.tile([P, PACK, P], F32, tag="turned")
+        turn_rows(nc, w_turned, w_rows_f, identity[:])
+        w_grouped = const.tile([P, P, PACK], BF16, align_bytes=64)
+        nc.vector.tensor_copy(out=w_grouped[:], in_=w_turned[:].rearrange("p j r -> p r j"))
+        w_codes = const.tile([P, WIDTH], U32, align_bytes=64)
+        w_scales = const.tile([P, WIDTH], U8, align_bytes=64)
+        nc.vector.quantize_mx(
+            out=w_codes[:].bitcast(FP8X4),
+            scales=w_scales[:],
+            in_=w_grouped[:].rearrange("p r j -> p (r j)"),
+        )
+
+        minus_means = {}
+        square_sums = {}
+        rstds = {}
+        turneds = {}
+        groupeds = {}
+        words = {}
+        projs = {}
+        gelus = {}
+
+        def sums(q):
+            if not 0 <= q < QUADS:
+                return
+            sum_vector = stat_pool.tile([P, QUAD // 2], F32)
+            sum_scalar = stat_pool.tile([P, QUAD // 2], F32)
+            for i in range(QUAD // 2):
+                unread_v = unread_pool.tile([P, DIM], BF16)
+                nc.vector.tensor_scalar(
+                    out=unread_v[:],
+                    in0=x_quads[q][:, i, :],
+                    scalar1=1.0,
+                    scalar2=None,
+                    op0=ALU.mult,
+                    op1=ALU.add,
+                    accum_out=sum_vector[:, i : i + 1],
+                )
+                unread_s = unread_pool.tile([P, DIM], BF16)
+                nc.scalar.activation(
+                    out=unread_s[:],
+                    in_=x_quads[q][:, QUAD // 2 + i, :],
+                    func=ACT.Identity,
+                    accum_out=sum_scalar[:, i : i + 1],
+                )
+            minus_mean = stat_pool.tile([P, QUAD], F32)
+            nc.vector.tensor_scalar_mul(out=minus_mean[:, 0 : QUAD // 2], in0=sum_vector[:], scalar1=-1.0 / DIM)
+            nc.vector.tensor_scalar_mul(out=minus_mean[:, QUAD // 2 : QUAD], in0=sum_scalar[:], scalar1=-1.0 / DIM)
+            minus_means[q] = minus_mean
+
+        def squares(q):
+            if not 0 <= q < QUADS:
+                return
+            square_sum = stat_pool.tile([P, QUAD], F32)
+            for i in range(QUAD):
+                unread_s = unread_pool.tile([P, DIM], BF16)
+                nc.scalar.activation(
+                    out=unread_s[:],
+                    in_=x_quads[q][:, i, :],
+                    func=ACT.Square,
+                    bias=minus_means[q][:, i : i + 1],
+                    accum_out=square_sum[:, i : i + 1],
+                )
+            square_sums[q] = square_sum
+
+        def inverse_std(q):
+            if not 0 <= q < QUADS:
+                return
+            var_eps = stat_pool.tile([P, QUAD], F32)
+            nc.vector.tensor_scalar(
+                out=var_eps[:], in0=square_sums[q][:], scalar1=1.0 / DIM, scalar2=EPS, op0=ALU.mult, op1=ALU.add
+            )
+            rstd = stat_pool.tile([P, QUAD], F32)
+            nc.gpsimd.tensor_tensor(out=rstd[:], in0=var_eps[:], in1=minus_half[:], op=ALU.pow)
+            rstds[q] = rstd
+
+        def normalise(q):
+            if not 0 <= q < QUADS:
+                return
+            for i in range(QUAD):
+                y = y_pool.tile([P, DIM], F32)
+                nc.gpsimd.tensor_scalar(
+                    out=y[:],
+                    in0=x_quads[q][:, i, :],
+                    scalar1=minus_means[q][:, i : i + 1],
+                    scalar2=rstds[q][:, i : i + 1],
+                    op0=ALU.add,
+                    op1=ALU.mult,
+                )
+                turned = turned_pool.tile([P, PACK, P], F32, tag="turned")
+                turn_rows(nc, turned, y, identity[:])
+                turneds[(q, i)] = turned
+
+        def apply_gain(q):
+            if not 0 <= q < QUADS:
+                return
+            grouped = mx_pool.tile([P, QUAD, P, PACK], BF16, align_bytes=64)
+            for i in range(QUAD):
+                nc.vector.tensor_tensor(
+                    out=grouped[:, i, :, :],
+                    in0=turneds[(q, i)][:].rearrange("p j r -> p r j"),
+                    in1=gain[:].unsqueeze(1).to_broadcast([P, P, PACK]),
+                    op=ALU.mult,
+                )
+            groupeds[q] = grouped
+
+        def quantise(q):
+            if not 0 <= q < QUADS:
+                return
+            codes = mx_pool.tile([P, QUAD * P], U32, align_bytes=64)
+            scales = mx_pool.tile([P, QUAD * P], U8, align_bytes=64)
+            nc.vector.quantize_mx(
+                out=codes[:].bitcast(FP8X4),
+                scales=scales[:],
+                in_=groupeds[q][:].rearrange("p i r j -> p (i r j)"),
+            )
+            words[q] = (codes, scales)
+
+        def project(q):
+            if not 0 <= q < QUADS:
+                return
+            codes, scales = words[q]
+            proj = proj_pool.tile([P, QUAD, WIDTH], F32)
+            for i in range(QUAD):
+                tokens = slice(i * P, (i + 1) * P)
+                nc.tensor.matmul_mx(
+                    out=proj[:, i, :],
+                    lhsT=codes[:, tokens].bitcast(FP8X4),
+                    lhsT_scale=scales[:, tokens],
+                    rhs=w_codes[:].bitcast(FP8X4),
+                    rhs_scale=w_scales[:],
+                    start=True,
+                    stop=True,
+                )
+            projs[q] = proj
+
+        def copy_and_gelu(q):
+            if not 0 <= q < QUADS:
+                return
+            tiles = slice(q * QUAD, (q + 1) * QUAD)
+            qk = out_pool.tile([P, 2, QUAD, QK], F32)
+            nc.scalar.copy(
+                out=qk[:].rearrange("p s i c -> p i s c"),
+                in_=projs[q][:, :, 0 : 2 * QK].rearrange("p i (s c) -> p i s c", s=2),
+            )
+            gelu_pre = out_pool.tile([P, QUAD, EXP], F32)
+            nc.scalar.activation(out=gelu_pre[:], in_=projs[q][:, :, 2 * QK + EXP : WIDTH], func=ACT.Gelu)
+            gelus[q] = gelu_pre
+            nc.sync.dma_start(out=q_rows[:, tiles, :], in_=qk[:, 0, :, :])
+            nc.sync.dma_start(out=k_rows[:, tiles, :], in_=qk[:, 1, :, :])
+
+        def gate(q):
+            if not 0 <= q < QUADS:
+                return
+            tiles = slice(q * QUAD, (q + 1) * QUAD)
+            glv = out_pool.tile([P, 2, QUAD, HALF_EXP], F32)
+            nc.vector.tensor_tensor(
+                out=glv[:].rearrange("p s i c -> p i s c"),
+                in0=projs[q][:, :, 2 * QK : 2 * QK + EXP].rearrange("p i (s c) -> p i s c", s=2),
+                in1=gelus[q][:].rearrange("p i (s c) -> p i s c", s=2),
+                op=ALU.mult,
+            )
+            nc.sync.dma_start(out=gl_rows[:, tiles, :], in_=glv[:, 0, :, :])
+            nc.sync.dma_start(out=gv_rows[:, tiles, :], in_=glv[:, 1, :, :])
+
+        with tc.manual_schedule():
+            for step in range(QUADS + 5):
+                inverse_std(step - 2)
+                project(step - 5)
+                apply_gain(step - 4)
+                normalise(step - 3)
+                sums(step)
+                copy_and_gelu(step - 5)
+                quantise(step - 4)
+                squares(step - 1)
+                gate(step - 5)

@@ -156,7 +156,8 @@ def tile_latentattentionblock_pa_t_kernel(tc, x, norm_w, expand_w, out_0, out_1,
                 return
             for i in range(QUAD):
                 y = y_pool.tile([P, DIM], F32)
-                nc.gpsimd.tensor_scalar(
+                engine = nc.gpsimd if i % 2 == 0 else nc.vector
+                engine.tensor_scalar(
                     out=y[:],
                     in0=x_quads[q][:, i, :],
                     scalar1=minus_means[q][:, i : i + 1],

@@ -100,42 +100,41 @@ def tile_latentattentionblock_pa_t_kernel(tc, x, norm_w, expand_w, out_0, out_1,
         def sums(q):
             if not 0 <= q < QUADS:
                 return
-            sum_vector = stat_pool.tile([P, QUAD // 2], F32)
-            sum_scalar = stat_pool.tile([P, QUAD // 2], F32)
+            by_vector = stat_pool.tile([P, QUAD // 2], F32)
+            by_scalar = stat_pool.tile([P, QUAD // 2], F32)
             for i in range(QUAD // 2):
                 unread_v = unread_pool.tile([P, DIM], BF16)
                 nc.vector.tensor_scalar(
                     out=unread_v[:],
                     in0=x_quads[q][:, i, :],
-                    scalar1=1.0,
+                    scalar1=-1.0 / DIM,
                     scalar2=None,
                     op0=ALU.mult,
                     op1=ALU.add,
-                    accum_out=sum_vector[:, i : i + 1],
+                    accum_out=by_vector[:, i : i + 1],
                 )
+                minus_means[(q, i)] = by_vector[:, i : i + 1]
                 unread_s = unread_pool.tile([P, DIM], BF16)
                 nc.scalar.activation(
                     out=unread_s[:],
                     in_=x_quads[q][:, QUAD // 2 + i, :],
                     func=ACT.Identity,
-                    accum_out=sum_scalar[:, i : i + 1],
+                    scale=-1.0 / DIM,
+                    accum_out=by_scalar[:, i : i + 1],
                 )
-            minus_mean = stat_pool.tile([P, QUAD], F32)
-            nc.vector.tensor_scalar_mul(out=minus_mean[:, 0 : QUAD // 2], in0=sum_vector[:], scalar1=-1.0 / DIM)
-            nc.vector.tensor_scalar_mul(out=minus_mean[:, QUAD // 2 : QUAD], in0=sum_scalar[:], scalar1=-1.0 / DIM)
-            minus_means[q] = minus_mean
+                minus_means[(q, QUAD // 2 + i)] = by_scalar[:, i : i + 1]
 
         def squares(q):
             if not 0 <= q < QUADS:
                 return
             square_sum = stat_pool.tile([P, QUAD], F32)
-            for i in range(QUAD):
+            for i in list(range(QUAD // 2, QUAD)) + list(range(QUAD // 2)):
                 unread_s = unread_pool.tile([P, DIM], BF16)
                 nc.scalar.activation(
                     out=unread_s[:],
                     in_=x_quads[q][:, i, :],
                     func=ACT.Square,
-                    bias=minus_means[q][:, i : i + 1],
+                    bias=minus_means[(q, i)],
                     accum_out=square_sum[:, i : i + 1],
                 )
             square_sums[q] = square_sum
@@ -160,7 +159,7 @@ def tile_latentattentionblock_pa_t_kernel(tc, x, norm_w, expand_w, out_0, out_1,
                 engine.tensor_scalar(
                     out=y[:],
                     in0=x_quads[q][:, i, :],
-                    scalar1=minus_means[q][:, i : i + 1],
+                    scalar1=minus_means[(q, i)],
                     scalar2=rstds[q][:, i : i + 1],
                     op0=ALU.add,
                     op1=ALU.mult,
@@ -242,13 +241,13 @@ def tile_latentattentionblock_pa_t_kernel(tc, x, norm_w, expand_w, out_0, out_1,
             nc.sync.dma_start(out=gv_rows[:, tiles, :], in_=glv[:, 1, :, :])
 
         with tc.manual_schedule():
-            for step in range(QUADS + 5):
-                inverse_std(step - 2)
-                project(step - 5)
-                apply_gain(step - 4)
-                normalise(step - 3)
+            for step in range(QUADS + 4):
+                apply_gain(step - 3)
+                normalise(step - 2)
+                inverse_std(step - 1)
+                quantise(step - 3)
+                project(step - 3)
                 sums(step)
-                copy_and_gelu(step - 5)
-                quantise(step - 4)
-                squares(step - 1)
-                gate(step - 5)
+                squares(step)
+                copy_and_gelu(step - 3)
+                gate(step - 4)

@@ -45,7 +45,7 @@ def tile_latentattentionblock_pa_t_kernel(tc, x, norm_w, expand_w, out_0, out_1,
         x_pool = ctx.enter_context(tc.tile_pool(name="x", bufs=QUADS))
         stat_pool = ctx.enter_context(tc.tile_pool(name="stat", bufs=6))
         unread_pool = ctx.enter_context(tc.tile_pool(name="unread", bufs=6))
-        y_pool = ctx.enter_context(tc.tile_pool(name="y", bufs=8))
+        y_pool = ctx.enter_context(tc.tile_pool(name="y", bufs=2 * QUAD))
         mx_pool = ctx.enter_context(tc.tile_pool(name="mx", bufs=3))
         out_pool = ctx.enter_context(tc.tile_pool(name="out", bufs=4))
         turned_pool = ctx.enter_context(tc.psum_pool(name="turned", bufs=6))
@@ -93,7 +93,7 @@ def tile_latentattentionblock_pa_t_kernel(tc, x, norm_w, expand_w, out_0, out_1,
         rstds = {}
         turneds = {}
         groupeds = {}
-        words = {}
+        quantised = {}
         projs = {}
         gelus = {}
 
@@ -155,7 +155,7 @@ def tile_latentattentionblock_pa_t_kernel(tc, x, norm_w, expand_w, out_0, out_1,
                 return
             for i in range(QUAD):
                 y = y_pool.tile([P, DIM], F32)
-                engine = nc.gpsimd if i % 2 == 0 else nc.vector
+                engine = nc.gpsimd if i < QUAD - 1 else nc.vector
                 engine.tensor_scalar(
                     out=y[:],
                     in0=x_quads[q][:, i, :],
@@ -191,12 +191,12 @@ def tile_latentattentionblock_pa_t_kernel(tc, x, norm_w, expand_w, out_0, out_1,
                 scales=scales[:],
                 in_=groupeds[q][:].rearrange("p i r j -> p (i r j)"),
             )
-            words[q] = (codes, scales)
+            quantised[q] = (codes, scales)
 
         def project(q):
             if not 0 <= q < QUADS:
                 return
-            codes, scales = words[q]
+            codes, scales = quantised[q]
             proj = proj_pool.tile([P, QUAD, WIDTH], F32)
             for i in range(QUAD):
                 tokens = slice(i * P, (i + 1) * P)

from contextlib import ExitStack

import concourse.mybir as mybir
from concourse.masks import make_identity

F32 = mybir.dt.float32
BF16 = mybir.dt.bfloat16
U32 = mybir.dt.uint32
U8 = mybir.dt.uint8
FP8X4 = mybir.dt.float8_e4m3fn_x4
ALU = mybir.AluOpType
ACT = mybir.ActivationFunctionType

P = 128
PACK = 4
TOKENS = 16 * 1024
DIM = 512
QK = 32
EXP = 32
HALF_EXP = 16
WIDTH = 2 * QK + 2 * EXP
EPS = 1e-5
TILES = TOKENS // P
QUAD = 4
QUADS = TILES // QUAD

FLOPS = 2 * TOKENS * DIM * WIDTH


def turn_rows(nc, turned, rows, identity):
    for j in range(PACK):
        nc.tensor.transpose(turned[:, j, :], rows[:, j * P : (j + 1) * P], identity)


def tile_latentattentionblock_pa_t_kernel(tc, x, norm_w, expand_w, out_0, out_1, out_2, out_3):
    nc = tc.nc
    x_rows = x.flatten_outer_dims().rearrange("(p i) d -> p i d", p=P)
    q_rows = out_0.flatten_outer_dims().rearrange("(p i) c -> p i c", p=P)
    k_rows = out_1.flatten_outer_dims().rearrange("(p i) c -> p i c", p=P)
    gl_rows = out_2.flatten_outer_dims().rearrange("(p i) c -> p i c", p=P)
    gv_rows = out_3.flatten_outer_dims().rearrange("(p i) c -> p i c", p=P)

    with ExitStack() as ctx:
        const = ctx.enter_context(tc.tile_pool(name="const", bufs=1))
        x_pool = ctx.enter_context(tc.tile_pool(name="x", bufs=QUADS))
        stat_pool = ctx.enter_context(tc.tile_pool(name="stat", bufs=6))
        unread_pool = ctx.enter_context(tc.tile_pool(name="unread", bufs=6))
        y_pool = ctx.enter_context(tc.tile_pool(name="y", bufs=2 * QUAD))
        mx_pool = ctx.enter_context(tc.tile_pool(name="mx", bufs=3))
        out_pool = ctx.enter_context(tc.tile_pool(name="out", bufs=4))
        turned_pool = ctx.enter_context(tc.psum_pool(name="turned", bufs=6))
        proj_pool = ctx.enter_context(tc.psum_pool(name="proj", bufs=2))

        w_rows = const.tile([P, DIM], BF16)
        nc.scalar.dma_start(out=w_rows[:], in_=expand_w)
        gain_rows = const.tile([P, P], BF16)
        nc.vector.memset(gain_rows[:], 0.0)
        nc.scalar.dma_start(out=gain_rows[0:PACK, :], in_=norm_w.rearrange("(j c) -> j c", c=P))
        x_quads = []
        for q in range(QUADS):
            x_quad = x_pool.tile([P, QUAD, DIM], BF16)
            nc.sync.dma_start(out=x_quad[:], in_=x_rows[:, q * QUAD : (q + 1) * QUAD, :])
            x_quads.append(x_quad)

        identity = const.tile([P, P], F32)
        make_identity(nc, identity[:])
        minus_half = const.tile([P, QUAD], F32)
        nc.vector.memset(minus_half[:], -0.5)

        gain_rows_f = const.tile([P, P], F32)
        nc.vector.tensor_copy(out=gain_rows_f[:], in_=gain_rows[:])
        gain_turned = turned_pool.tile([P, PACK, P], F32, tag="turned")
        nc.tensor.transpose(gain_turned[:, 0, :], gain_rows_f[:], identity[:])
        gain = const.tile([P, PACK], F32)
        nc.vector.tensor_copy(out=gain[:], in_=gain_turned[:, 0, 0:PACK])

        w_rows_f = const.tile([P, DIM], F32)
        nc.vector.tensor_copy(out=w_rows_f[:], in_=w_rows[:])
        w_turned = turned_pool.tile([P, PACK, P], F32, tag="turned")
        turn_rows(nc, w_turned, w_rows_f, identity[:])
        w_grouped = const.tile([P, P, PACK], BF16, align_bytes=64)
        nc.vector.tensor_copy(out=w_grouped[:], in_=w_turned[:].rearrange("p j r -> p r j"))
        w_codes = const.tile([P, WIDTH], U32, align_bytes=64)
        w_scales = const.tile([P, WIDTH], U8, align_bytes=64)
        nc.vector.quantize_mx(
            out=w_codes[:].bitcast(FP8X4),
            scales=w_scales[:],
            in_=w_grouped[:].rearrange("p r j -> p (r j)"),
        )

        minus_means = {}
        square_sums = {}
        rstds = {}
        turneds = {}
        groupeds = {}
        quantised = {}
        projs = {}
        gelus = {}

        def sums(q):
            if not 0 <= q < QUADS:
                return
            by_vector = stat_pool.tile([P, QUAD // 2], F32)
            by_scalar = stat_pool.tile([P, QUAD // 2], F32)
            for i in range(QUAD // 2):
                unread_v = unread_pool.tile([P, DIM], BF16)
                nc.vector.tensor_scalar(
                    out=unread_v[:],
                    in0=x_quads[q][:, i, :],
                    scalar1=-1.0 / DIM,
                    scalar2=None,
                    op0=ALU.mult,
                    op1=ALU.add,
                    accum_out=by_vector[:, i : i + 1],
                )
                minus_means[(q, i)] = by_vector[:, i : i + 1]
                unread_s = unread_pool.tile([P, DIM], BF16)
                nc.scalar.activation(
                    out=unread_s[:],
                    in_=x_quads[q][:, QUAD // 2 + i, :],
                    func=ACT.Identity,
                    scale=-1.0 / DIM,
                    accum_out=by_scalar[:, i : i + 1],
                )
                minus_means[(q, QUAD // 2 + i)] = by_scalar[:, i : i + 1]

        def squares(q):
            if not 0 <= q < QUADS:
                return
            square_sum = stat_pool.tile([P, QUAD], F32)
            for i in list(range(QUAD // 2, QUAD)) + list(range(QUAD // 2)):
                unread_s = unread_pool.tile([P, DIM], BF16)
                nc.scalar.activation(
                    out=unread_s[:],
                    in_=x_quads[q][:, i, :],
                    func=ACT.Square,
                    bias=minus_means[(q, i)],
                    accum_out=square_sum[:, i : i + 1],
                )
            square_sums[q] = square_sum

        def inverse_std(q):
            if not 0 <= q < QUADS:
                return
            var_eps = stat_pool.tile([P, QUAD], F32)
            nc.vector.tensor_scalar(
                out=var_eps[:], in0=square_sums[q][:], scalar1=1.0 / DIM, scalar2=EPS, op0=ALU.mult, op1=ALU.add
            )
            rstd = stat_pool.tile([P, QUAD], F32)
            nc.gpsimd.tensor_tensor(out=rstd[:], in0=var_eps[:], in1=minus_half[:], op=ALU.pow)
            rstds[q] = rstd

        def normalise(q):
            if not 0 <= q < QUADS:
                return
            for i in range(QUAD):
                y = y_pool.tile([P, DIM], F32)
                engine = nc.gpsimd if i < QUAD - 1 else nc.vector
                engine.tensor_scalar(
                    out=y[:],
                    in0=x_quads[q][:, i, :],
                    scalar1=minus_means[(q, i)],
                    scalar2=rstds[q][:, i : i + 1],
                    op0=ALU.add,
                    op1=ALU.mult,
                )
                turned = turned_pool.tile([P, PACK, P], F32, tag="turned")
                turn_rows(nc, turned, y, identity[:])
                turneds[(q, i)] = turned

        def apply_gain(q):
            if not 0 <= q < QUADS:
                return
            grouped = mx_pool.tile([P, QUAD, P, PACK], BF16, align_bytes=64)
            for i in range(QUAD):
                nc.vector.tensor_tensor(
                    out=grouped[:, i, :, :],
                    in0=turneds[(q, i)][:].rearrange("p j r -> p r j"),
                    in1=gain[:].unsqueeze(1).to_broadcast([P, P, PACK]),
                    op=ALU.mult,
                )
            groupeds[q] = grouped

        def quantise(q):
            if not 0 <= q < QUADS:
                return
            codes = mx_pool.tile([P, QUAD * P], U32, align_bytes=64)
            scales = mx_pool.tile([P, QUAD * P], U8, align_bytes=64)
            nc.vector.quantize_mx(
                out=codes[:].bitcast(FP8X4),
                scales=scales[:],
                in_=groupeds[q][:].rearrange("p i r j -> p (i r j)"),
            )
            quantised[q] = (codes, scales)

        def project(q):
            if not 0 <= q < QUADS:
                return
            codes, scales = quantised[q]
            proj = proj_pool.tile([P, QUAD, WIDTH], F32)
            for i in range(QUAD):
                tokens = slice(i * P, (i + 1) * P)
                nc.tensor.matmul_mx(
                    out=proj[:, i, :],
                    lhsT=codes[:, tokens].bitcast(FP8X4),
                    lhsT_scale=scales[:, tokens],
                    rhs=w_codes[:].bitcast(FP8X4),
                    rhs_scale=w_scales[:],
                    start=True,
                    stop=True,
                )
            projs[q] = proj

        def copy_and_gelu(q):
            if not 0 <= q < QUADS:
                return
            tiles = slice(q * QUAD, (q + 1) * QUAD)
            qk = out_pool.tile([P, 2, QUAD, QK], F32)
            nc.scalar.copy(
                out=qk[:].rearrange("p s i c -> p i s c"),
                in_=projs[q][:, :, 0 : 2 * QK].rearrange("p i (s c) -> p i s c", s=2),
            )
            gelu_pre = out_pool.tile([P, QUAD, EXP], F32)
            nc.scalar.activation(out=gelu_pre[:], in_=projs[q][:, :, 2 * QK + EXP : WIDTH], func=ACT.Gelu)
            gelus[q] = gelu_pre
            nc.sync.dma_start(out=q_rows[:, tiles, :], in_=qk[:, 0, :, :])
            nc.sync.dma_start(out=k_rows[:, tiles, :], in_=qk[:, 1, :, :])

        def gate(q):
            if not 0 <= q < QUADS:
                return
            tiles = slice(q * QUAD, (q + 1) * QUAD)
            glv = out_pool.tile([P, 2, QUAD, HALF_EXP], F32)
            nc.vector.tensor_tensor(
                out=glv[:].rearrange("p s i c -> p i s c"),
                in0=projs[q][:, :, 2 * QK : 2 * QK + EXP].rearrange("p i (s c) -> p i s c", s=2),
                in1=gelus[q][:].rearrange("p i (s c) -> p i s c", s=2),
                op=ALU.mult,
            )
            nc.sync.dma_start(out=gl_rows[:, tiles, :], in_=glv[:, 0, :, :])
            nc.sync.dma_start(out=gv_rows[:, tiles, :], in_=glv[:, 1, :, :])

        with tc.manual_schedule():
            for step in range(QUADS + 4):
                apply_gain(step - 3)
                normalise(step - 2)
                inverse_std(step - 1)
                quantise(step - 3)
                project(step - 3)
                sums(step)
                squares(step)
                copy_and_gelu(step - 3)
                gate(step - 4)
